import numpy as np
import ml_dtypes


def mxq(x, axis, fmt="e4m3"):
    dtype, down = {"e4m3": (ml_dtypes.float8_e4m3fn, 7), "e5m2": (ml_dtypes.float8_e5m2, 14)}[fmt]
    v = np.moveaxis(np.asarray(x, np.float32).astype(ml_dtypes.bfloat16).astype(np.float64), axis, -1)
    blocks = v.reshape(v.shape[:-1] + (-1, 32))
    amax = np.abs(blocks).max(-1, keepdims=True)
    byte = np.maximum(np.where(amax > 0, np.frexp(amax)[1] - 1 + 127, 0) - down, 1)
    scale = np.exp2(byte - 127.0)
    codes = (blocks / scale).astype(np.float32).astype(dtype).astype(np.float64)
    return np.moveaxis((codes * scale).reshape(v.shape), -1, axis)


WIDE = False


def mx_kscale(k):
    if not WIDE:
        return np.ones(k)
    levels = np.array([10, -10, 5, -5, 0])
    if k % 512:
        return np.exp2(np.random.permutation(np.resize(levels, k // 32))).repeat(32)
    a = np.empty((k // 512, 16))
    for p in range(k // 512):
        a[p, :8] = np.random.permutation(np.resize(levels, 8))
        for g in range(8):
            far = levels[np.abs(levels - a[p, g]) >= 10]
            a[p, g + 8] = far[np.random.randint(len(far))]
    return np.exp2(a.ravel()).repeat(32)


BF16 = ml_dtypes.bfloat16


def bf(x):
    return np.asarray(x, np.float32).astype(BF16)


def f64(x):
    return np.asarray(x).astype(np.float64)


B, C, CP, H, W, KW = 1, 512, 19, 48, 48, 7
PAD = KW // 2
BN_EPS = 1e-5


def pad_hw(v):
    return np.pad(v, ((0, 0), (0, 0), (PAD, PAD), (PAD, PAD)))


def draw0():
    s, t = mx_kscale(C), mx_kscale(C)
    return {
        "x": bf(np.random.standard_normal((B, C, H, W))),
        "coarse_probs": bf(np.random.random((B, CP, H, W))),
        "sigma": bf(1.5 + 0.1 * np.random.standard_normal(1)),
        "w_feat": bf(np.random.standard_normal((C, C)) * 2.0 / np.sqrt(C) * t[:, None] / s[None, :]),
        "w_fuse": bf(np.random.standard_normal((C, C)) * 2.5 / np.sqrt(C) / t[None, :]),
        "bn_gamma": bf((1.0 + 0.1 * np.random.standard_normal(C)) * s),
        "bn_beta": bf(0.1 * np.random.standard_normal(C) * s),
        "bn_mean": bf(0.1 * np.random.standard_normal(C)),
        "bn_var": bf(np.random.random(C) + 0.5),
    }


def core(x, coarse_probs, sigma, w_feat, w_fuse, bn_gamma, bn_beta, bn_mean, bn_var):
    x, p = f64(x), f64(coarse_probs)
    inv = 1.0 / np.sqrt(f64(bn_var) + BN_EPS)
    xn = (x - f64(bn_mean)[None, :, None, None]) * (inv * f64(bn_gamma))[None, :, None, None] + f64(bn_beta)[None, :, None, None]

    pp = pad_hw(p)
    dist_sq = np.stack([((pp[:, :, i:i + H, j:j + W] - p) ** 2).sum(axis=1) for i in range(KW) for j in range(KW)], axis=1)
    denom = 2.0 * np.maximum(f64(sigma)[0], 0.0) ** 2 + 1e-8
    a = np.exp(-dist_sq / denom)
    e = np.exp(a - a.max(axis=1, keepdims=True))
    affinity = e / e.sum(axis=1, keepdims=True)

    xq = mxq(xn, 1, "e4m3")
    messages = (mxq(f64(w_feat), 1, "e4m3") @ xq.reshape(B, C, H * W)).reshape(B, C, H, W)

    mp = pad_hw(messages)
    agg = np.zeros((B, C, H, W))
    for i in range(KW):
        for j in range(KW):
            agg = agg + mp[:, :, i:i + H, j:j + W] * affinity[:, i * KW + j][:, None]

    aq = mxq(agg, 1, "e4m3")
    refined = (mxq(f64(w_fuse), 1, "e4m3") @ aq.reshape(B, C, H * W)).reshape(B, C, H, W)
    return x + refined


def e4m3fn_bytes(y):
    return np.clip(np.asarray(y, np.float64), -448.0, 448.0).astype(np.float32).astype(ml_dtypes.float8_e4m3fn).view(np.uint8)


def e4m3fn_values(b):
    return np.asarray(b, np.uint8).view(ml_dtypes.float8_e4m3fn).astype(np.float64)


def setup_inputs():
    d = draw0()
    x0 = np.asarray(d['w_fuse']).astype(np.float64)
    s = (np.max(np.abs(x0), axis=(0,), keepdims=True) / 448.0).astype(np.float32)
    out = {}
    for k, v in d.items():
        if k == 'w_fuse':
            out['w_fuse_bytes'] = e4m3fn_bytes(x0 / s.astype(np.float64))
            out['w_fuse_scale'] = s
        else:
            out[k] = v
    return out


def reference(x, coarse_probs, sigma, w_feat, w_fuse_bytes, w_fuse_scale, bn_gamma, bn_beta, bn_mean, bn_var):
    return core(x, coarse_probs, sigma, w_feat, e4m3fn_values(w_fuse_bytes) * w_fuse_scale.astype(np.float64), bn_gamma, bn_beta, bn_mean, bn_var)

from contextlib import ExitStack

import concourse.mybir as mybir
from concourse.masks import make_identity

F32 = mybir.dt.float32
BF16 = mybir.dt.bfloat16
U8 = mybir.dt.uint8
U32 = mybir.dt.uint32
I32 = mybir.dt.int32
FP8 = mybir.dt.float8_e4m3fn
FP8X4 = mybir.dt.float8_e4m3fn_x4
ACT = mybir.ActivationFunctionType
ALU = mybir.AluOpType
AX = mybir.AxisListType

C, H, W, CP = 512, 48, 48, 19
P, T = 128, 4
TAPS = 49
NPIX = H * W
BANDS, WROWS = 8, 10
CHUNK = 256
FLOPS = 2 * 2 * C * C * NPIX + 2 * TAPS * C * NPIX


def tile_dcblock_kernel(
    tc, x, coarse_probs, sigma, w_feat, w_fuse_bytes, w_fuse_scale, bn_gamma, bn_beta, bn_mean, bn_var, out
):
    nc = tc.nc
    with ExitStack() as ctx:
        one = ctx.enter_context(tc.tile_pool(name="one", bufs=1))
        two = ctx.enter_context(tc.tile_pool(name="two", bufs=2))
        four = ctx.enter_context(tc.tile_pool(name="four", bufs=4))
        psum_win = ctx.enter_context(tc.psum_pool(name="psum_win", bufs=2))
        psum_v = ctx.enter_context(tc.psum_pool(name="psum_v", bufs=2))
        psum_agg = ctx.enter_context(tc.psum_pool(name="psum_agg", bufs=2))
        psum_out = ctx.enter_context(tc.psum_pool(name="psum_out", bufs=2))

        pg = one.tile([P, 12 * 72], BF16, name="pg", align_bytes=64)
        pv = one.tile([P, 12, 64], BF16, name="pv", align_bytes=64)
        nc.gpsimd.memset(pg[:].bitcast(F32), 0.0)
        nc.gpsimd.memset(pv[:].rearrange("p r c -> p (r c)").bitcast(F32), 0.0)
        ident_b = one.tile([P, P], BF16, name="ident_b")
        make_identity(nc, ident_b[:])
        ident_f = one.tile([P, P], F32, name="ident_f")
        make_identity(nc, ident_f[:])
        xvf = one.tile([P, 16, 64, T], BF16, name="xvf", align_bytes=64)
        nc.gpsimd.memset(xvf[:].rearrange("p r c t -> p (r c t)").bitcast(F32), 0.0)
        et = one.tile([P, 25 * P], F32, name="et")
        nc.gpsimd.memset(et[:], 0.0)

        cp = coarse_probs.rearrange("o c h w -> (o c) h w")
        pg4 = pg[:].rearrange("p (r c) -> p r c", c=72)
        for i in range(6):
            ps, pe = i * CP, (i + 1) * CP
            n = min(11, 13 - i)
            nc.sync.dma_start(out=pv[ps:pe, 0:n, 4:52], in_=cp[:, 35 + i : 35 + i + n, :])
        for i in range(6):
            ps, pe = i * CP, (i + 1) * CP
            r0 = 1 if i < 3 else 0
            h0 = 4 * r0 + i - 3
            nr = 11 - r0
            nc.sync.dma_start(out=pg4[ps:pe, r0:11, 4:52], in_=cp[:, h0 : h0 + 4 * (nr - 1) + 1 : 4, :])

        par = []
        for name, v in (("gamma", bn_gamma), ("beta", bn_beta), ("mean", bn_mean), ("var", bn_var)):
            vec = one.tile([P, T], BF16, name=name)
            nc.scalar.dma_start(out=vec[:], in_=v.rearrange("(p t) -> p t", t=T))
            par.append(vec)
        sig = one.tile([P, 1], BF16, name="sig")
        nc.scalar.dma_start(out=sig[:], in_=sigma.partition_broadcast(P))
        xr = one.tile([P, T, H, W], BF16, name="xr", tag="raster", align_bytes=64)
        xin = x.rearrange("o (p t) h w -> (o p) t h w", t=T)
        for h0 in (32, 0, 16):
            nc.scalar.dma_start(out=xr[:, :, h0 : h0 + 16, :], in_=xin[:, :, h0 : h0 + 16, :])
        wf = two.tile([P, T, C], BF16, name="wf", tag="wrow", align_bytes=64)
        nc.sync.dma_start(out=wf[:], in_=w_feat.rearrange("(m t) k -> m t k", t=T))
        wb = one.tile([P, T, C], U8, name="wb", align_bytes=64)
        nc.sync.dma_start(out=wb[:], in_=w_fuse_bytes.rearrange("(m t) k -> m t k", t=T))
        sc = one.tile([P, C], F32, name="sc")
        nc.scalar.dma_start(out=sc[:], in_=w_fuse_scale.rearrange("o k -> (o k)").partition_broadcast(P))

        neg1 = one.tile([P, 1], F32, name="neg1")
        nc.vector.memset(neg1[:], -1.0)
        ninv = one.tile([P, 1], F32, name="ninv")
        sg = one.tile([P, 1], F32, name="sg")
        nc.vector.tensor_scalar(out=sg[:], in0=sig[:], scalar1=0.0, scalar2=None, op0=ALU.max)
        nc.vector.tensor_tensor(out=sg[:], in0=sg[:], in1=sg[:], op=ALU.mult)
        nc.vector.tensor_scalar(out=sg[:], in0=sg[:], scalar1=2.0, scalar2=1e-8, op0=ALU.mult, op1=ALU.add)
        nc.vector.reciprocal(out=sg[:], in_=sg[:])
        nc.vector.tensor_scalar(out=ninv[:], in0=sg[:], scalar1=-1.0, scalar2=None, op0=ALU.mult)
        gain = one.tile([P, T], F32, name="gain")
        shift = one.tile([P, T], F32, name="shift")
        nc.vector.tensor_scalar(out=gain[:], in0=par[3][:], scalar1=1e-5, scalar2=None, op0=ALU.add)
        nc.scalar.activation(out=gain[:], in_=gain[:], func=ACT.Sqrt)
        nc.vector.reciprocal(out=gain[:], in_=gain[:])
        nc.vector.tensor_tensor(out=gain[:], in0=gain[:], in1=par[0][:], op=ALU.mult)
        nc.vector.tensor_tensor(out=shift[:], in0=gain[:], in1=par[2][:], op=ALU.mult)
        nc.vector.tensor_tensor(out=shift[:], in0=par[1][:], in1=shift[:], op=ALU.subtract)

        pvc = one.tile([P, 9, 9, 16], BF16, name="pvc")
        pvf = pv[:].rearrange("p r c -> p (r c)")
        for s in range(9):
            nc.vector.tensor_copy(out=pvc[:, s], in_=pv[:, 0:9, 1 + s : 47 + s : 3])
        ppv = one.tile([P, 2, CP, 63], BF16, name="ppv")
        pp1 = ppv[:, 0].rearrange("p c (i j) -> p c i j", j=9)
        pp2 = ppv[:, 1].rearrange("p c (i j) -> p c i j", j=9)
        for dst, ncol, src in (
            (pp1, 9, lambda s, lo: pvc[:, s, lo : lo + 8, :].rearrange("p r c -> p (r c)")),
            (pp2, 7, lambda s, lo: pvf[:, (8 + lo) * 64 + 1 + s : (8 + lo) * 64 + 1 + s + P]),
        ):
            for s0 in range(0, ncol, 4):
                n = min(4, ncol - s0)
                for lo in (0, 1):
                    gp = psum_agg.tile([P, 4, P], BF16, name="gp", tag="agg")
                    for j in range(n):
                        nc.tensor.transpose(gp[:, j, :], src(s0 + j, lo), ident_b[:])
                    if lo == 0:
                        nc.scalar.copy(
                            out=dst[:, :, 0:6, s0 : s0 + n],
                            in_=gp[:, 0:n, 0:114].rearrange("w s (i c) -> w c i s", c=CP),
                        )
                    else:
                        nc.scalar.copy(
                            out=dst[:, :, 6, s0 : s0 + n], in_=gp[:, 0:n, 95:114].rearrange("w s c -> w c s")
                        )
        ppg = one.tile([P, CP, 10, 12], BF16, name="ppg")
        for s0 in (0, 4, 8):
            for lo in (0, 1):
                gp = psum_agg.tile([P, 4, P], BF16, name="gp", tag="agg")
                for j in range(4):
                    off = 72 * lo + 1 + s0 + j
                    nc.tensor.transpose(gp[:, j, :], pg[:, off : off + 127 * 6 + 1 : 6], ident_b[:])
                if lo == 0:
                    nc.scalar.copy(
                        out=ppg[:, :, 0:6, s0 : s0 + 4], in_=gp[:, :, 0:114].rearrange("w s (i c) -> w c i s", c=CP)
                    )
                else:
                    nc.vector.tensor_copy(
                        out=ppg[:, :, 6:10, s0 : s0 + 4], in_=gp[:, :, 38:114].rearrange("w s (i c) -> w c i s", c=CP)
                    )
        npv = one.tile([P, CP, 4], F32, name="npv")
        nc.vector.tensor_scalar(out=npv[:, :, 0:3], in0=pp1[:, :, 3, 3:6], scalar1=-1.0, scalar2=None, op0=ALU.mult)
        nc.vector.tensor_scalar(out=npv[:, :, 3], in0=pp2[:, :, 3, 3], scalar1=-1.0, scalar2=None, op0=ALU.mult)
        npg = one.tile([P, CP, 4, 6], F32, name="npg")
        nc.vector.tensor_scalar(out=npg[:], in0=ppg[:, :, 3:7, 3:9], scalar1=-1.0, scalar2=None, op0=ALU.mult)

        for h0 in (32, 0, 16):
            for t in range(T):
                rows = xr[:, t, h0 : h0 + 16, :]
                nc.vector.tensor_scalar(
                    out=rows, in0=rows, scalar1=gain[:, t : t + 1], scalar2=shift[:, t : t + 1], op0=ALU.mult, op1=ALU.add
                )

        def affinity(nbr, ctr):
            sq = two.tile([P, 4, CP, TAPS], F32, name="sq")
            for k in range(4):
                for ch in range(CP):
                    nc.scalar.activation(
                        out=sq[:, k, ch, :].rearrange("p (i j) -> p i j", j=7), in_=nbr(k, ch), func=ACT.Square, bias=ctr(k, ch)
                    )
            for a, b, n in ((0, 9, 9), (0, 4, 4), (0, 2, 2), (0, 1, 1), (0, 8, 1), (0, 18, 1)):
                nc.vector.tensor_tensor(
                    out=sq[:, :, a : a + n, :], in0=sq[:, :, a : a + n, :], in1=sq[:, :, b : b + n, :], op=ALU.add
                )
            aff = two.tile([P, 4, TAPS], F32, name="aff")
            nc.scalar.activation(out=aff[:], in_=sq[:, :, 0, :], func=ACT.Exp, scale=ninv[:, 0:1])
            nc.scalar.activation(out=aff[:], in_=aff[:], func=ACT.Exp, bias=neg1[:, 0:1])
            rz = two.tile([P, 4], F32, name="rz")
            nc.vector.tensor_reduce(out=rz[:], in_=aff[:], axis=AX.X, op=ALU.add)
            nc.vector.reciprocal(out=rz[:], in_=rz[:])
            return aff, rz

        def nbr_v(k, ch):
            return pp1[:, ch, :, k : k + 7] if k < 3 else pp2[:, ch, :, 0:7]

        aff, rz = affinity(nbr_v, lambda k, ch: npv[:, ch, k : k + 1])
        ev = one.tile([P, 4, TAPS], F32, name="ev")
        nc.vector.tensor_tensor(
            out=ev[:], in0=aff[:], in1=rz[:].unsqueeze(2).to_broadcast([P, 4, TAPS]), op=ALU.mult
        )

        def stationary(src, codes, scales):
            grouped = one.tile([P, C, T], BF16, name="wgrouped", tag="wgrouped", align_bytes=64)
            words = src[:].rearrange("m t k -> m (t k)").bitcast(F32).rearrange("m (t k) -> m t k", t=T)
            gwords = grouped[:].rearrange("p c j -> p (c j)").bitcast(F32).rearrange("p (c u) -> p c u", u=2)
            for half in (0, 1):
                wps = psum_win.tile([P, 2, 2, P], F32, name="wps", tag="win")
                for a in (0, 1):
                    for u in (0, 1):
                        nc.tensor.transpose(wps[:, a, u, :], words[:, 2 * half + a, u:256:2], ident_f[:])
                nc.scalar.copy(
                    out=gwords[:, 256 * half : 256 * half + 256, :].rearrange("p (a r) u -> p a r u", a=2),
                    in_=wps[:].rearrange("p a u r -> p a r u"),
                )
            nc.vector.quantize_mx(out=codes[:].bitcast(FP8X4), scales=scales[:], in_=grouped[:].rearrange("p c j -> p (c j)"))

        w1c = one.tile([P, C], U32, name="w1c", align_bytes=64)
        w1s = one.tile([P, C], U8, name="w1s", align_bytes=64)
        stationary(wf, w1c, w1s)

        xvq = one.tile([P, 17, 64], U32, name="xvq", align_bytes=64)
        xvs = one.tile([P, 17 * 64], U8, name="xvs", align_bytes=64)
        nc.vector.memset(xvs[:].bitcast(I32), 0)
        nc.vector.memset(xvq[:, 16, :].bitcast(I32), 0)
        for r0, r1 in ((0, 12), (12, 13)):
            nc.vector.tensor_copy(
                out=xvf[:, r0:r1, 3:51, :], in_=xr[:, :, 35 + r0 : 35 + r1, :].rearrange("p t h w -> p h w t")
            )
        nc.vector.quantize_mx(
            out=xvq[:, 0:16, :].rearrange("p r c -> p (r c)").bitcast(FP8X4),
            scales=xvs[:, 0:1024],
            in_=xvf[:].rearrange("p r c t -> p (r c t)"),
        )
        xvqi = xvq[:].rearrange("p r c -> p (r c)").bitcast(I32)
        xvqi3 = xvqi.rearrange("p (r c) -> p r c", c=64)
        xvs3 = xvs[:].rearrange("p (r c) -> p r c", c=64)
        v1w = one.tile([P, 9, 14, 16], U32, name="v1w", align_bytes=64)
        v1p = one.tile([P, 4, 9, 256], U8, name="v1p", align_bytes=64)
        v1wi = v1w[:].rearrange("p s r c -> p (s r c)").bitcast(I32).rearrange("p (s r c) -> p s r c", s=9, c=16)
        v1pi = v1p[:].rearrange("p k s n -> p (k s n)").bitcast(I32).rearrange("p (k s n) -> p k s n", k=4, s=9)
        for s in range(9):
            nc.vector.tensor_copy(out=v1wi[:, s], in_=xvqi3[:, 0:14, s : s + 46 : 3])
            nc.vector.tensor_copy(
                out=v1p[:, 0, s, 0:224].rearrange("p (r c) -> p r c", c=16), in_=xvs3[:, 0:14, s : s + 46 : 3]
            )
        for k in (1, 2, 3):
            nc.vector.tensor_copy(out=v1pi[:, k, :, 0 : 56 - 4 * k], in_=v1pi[:, 0, :, 4 * k : 56])

        v2cache = {}

        def v2operands(s):
            if s not in v2cache:
                codes = two.tile([P, 512], U32, name="v2c", align_bytes=64)
                scales = two.tile([P, 512], U8, name="v2s", align_bytes=64)
                nc.vector.tensor_copy(out=codes[:].bitcast(I32), in_=xvqi[:, 512 + s : 1024 + s])
                nc.vector.tensor_copy(out=scales[:], in_=xvs[:, 512 + s : 1024 + s])
                v2cache[s] = (codes, scales)
            return v2cache[s]

        def v1unit(s, r):
            k = r % 4
            lhs = v1w[:, s, r : r + 8, :].rearrange("p r c -> p (r c)")
            off = 16 * (r - k)
            uses = [(e, 7 * r + s - e) for e in range(3) if 0 <= s - e < 7]
            return lhs, v1p[:, k, s, off : off + P], uses

        def v2unit(s, r):
            codes, scales = v2operands(s)
            return codes[:, 64 * r : 64 * r + P], scales[:, 64 * r : 64 * r + P], [(3, 7 * r + s)]

        units = []
        done2 = 0
        seq2 = [(s, r) for s in range(7) for r in range(7)]
        for n, (s, r) in enumerate([(s, r) for s in range(9) for r in range(7)]):
            units.append((v1unit, s, r))
            while done2 < (n + 1) * 49 // 63:
                units.append((v2unit,) + seq2[done2])
                done2 += 1

        acc = [[one.tile([P, C], F32, name="acc%d%d" % (g, e)) for e in range(4)] for g in range(2)]
        fresh = {(g, e): True for g in range(2) for e in range(4)}

        def strip_unit(unit, helper):
            lhs, lscale, uses = unit[0](unit[1], unit[2])
            vps = psum_v.tile([P, C], F32, name="vps")
            nc.tensor.matmul_mx(
                out=vps[:], lhsT=lhs.bitcast(FP8X4), lhsT_scale=lscale, rhs=w1c[:].bitcast(FP8X4), rhs_scale=w1s[:], start=True, stop=True
            )
            g = 1 if helper else 0
            for e, tap in uses:
                a = acc[g][e]
                s = ev[:, e, tap : tap + 1]
                if helper:
                    dst = a if fresh[g, e] else four.tile([P, C], F32, name="prod")
                    nc.scalar.activation(out=dst[:], in_=vps[:], func=ACT.Copy, scale=s)
                    if not fresh[g, e]:
                        nc.gpsimd.tensor_tensor(out=a[:], in0=a[:], in1=dst[:], op=ALU.add)
                elif fresh[g, e]:
                    nc.vector.tensor_scalar(out=a[:], in0=vps[:], scalar1=s, scalar2=None, op0=ALU.mult)
                else:
                    nc.vector.scalar_tensor_tensor(out=a[:], in0=vps[:], scalar=s, in1=a[:], op0=ALU.mult, op1=ALU.add)
                fresh[g, e] = False

        upos = 0

        xbq = one.tile([P, BANDS, 576], U32, name="xbq", align_bytes=64)
        xbs = one.tile([P, BANDS, 576], U8, name="xbs", align_bytes=64)
        nc.vector.memset(xbs[:].rearrange("p b n -> p (b n)").bitcast(I32), 0)
        for b in range(BANDS):
            lo = 3 if b == 0 else 0
            hi = 9 if b == BANDS - 1 else 12
            xb = two.tile([P, 48, 12, T], BF16, name="xb", align_bytes=64)
            nc.vector.memset(xb[:, 0:3], 0.0)
            nc.vector.memset(xb[:, 47:48], 0.0)
            if lo:
                nc.vector.memset(xb[:, 3:47, 0:lo, :], 0.0)
            if hi < 12:
                nc.vector.memset(xb[:, 3:47, hi:12, :], 0.0)
            nc.vector.tensor_copy(
                out=xb[:, 3:47, lo:hi, :],
                in_=xr[:, :, 0:44, 6 * b + lo - 3 : 6 * b + hi - 3].rearrange("p t h w -> p h w t"),
            )
            flat = xb[:].rearrange("p r c t -> p (r c t)")
            for n0, n1 in ((0, 512), (512, 576)):
                nc.vector.quantize_mx(
                    out=xbq[:, b, n0:n1].bitcast(FP8X4), scales=xbs[:, b, n0:n1], in_=flat[:, T * n0 : T * n1]
                )
        xbsi = xbs[:].rearrange("p b n -> p (b n)").bitcast(I32).rearrange("p (b n) -> p b n", b=BANDS)
        xbk = {}
        for k, n in ((1, 3), (2, 2), (3, 2)):
            shifted = one.tile([P, BANDS, n, P], U8, name="xbk%d" % k, align_bytes=64)
            si = shifted[:].rearrange("p b s n -> p (b s n)").bitcast(I32).rearrange("p (b s n) -> p b s n", b=BANDS, s=n)
            for s in range(n):
                nc.vector.tensor_copy(out=si[:, :, s, :], in_=xbsi[:, :, 12 * k + 48 * s : 12 * k + 48 * s + 32])
            xbk[k] = shifted

        eg = one.tile([P, WROWS, BANDS, 24], F32, name="eg")
        npg2 = npg[:].rearrange("p c r d -> p c (r d)")
        for g in range(6):
            aff, rz = affinity(
                lambda k, ch: ppg[:, ch, (4 * g + k) // 6 : (4 * g + k) // 6 + 7, (4 * g + k) % 6 : (4 * g + k) % 6 + 7],
                lambda k, ch: npg2[:, ch, 4 * g + k : 4 * g + k + 1],
            )
            k0 = 0
            while k0 < 4:
                dr, dc = divmod(4 * g + k0, 6)
                n = min(4 - k0, 6 - dc)
                base = P * (4 * g + k0) + 12 * dr + dc
                dst = (
                    et[:, base : base + 129 * n]
                    .rearrange("p (d z) -> p d z", z=129)[:, :, 0:84]
                    .rearrange("p d (i j) -> p d i j", j=12)[:, :, :, 0:7]
                )
                nc.vector.tensor_tensor(
                    out=dst,
                    in0=aff[:, k0 : k0 + n, :].rearrange("p d (i j) -> p d i j", j=7),
                    in1=rz[:, k0 : k0 + n].unsqueeze(2).unsqueeze(3).to_broadcast([P, n, 7, 7]),
                    op=ALU.mult,
                )
                k0 += n
            tp = psum_agg.tile([P, 4, P], F32, name="tp", tag="agg")
            for k in range(4):
                d = 4 * g + k
                nc.tensor.transpose(tp[:, k, :], et[:, P * d : P * d + P], ident_f[:])
            nc.vector.tensor_copy(
                out=eg[:, :, :, 4 * g : 4 * g + 4],
                in_=tp[:, :, 0:120].rearrange("s d (r b) -> s r b d", b=12)[:, :, 0:BANDS, :],
            )
            for unit in units[upos : upos + 5]:
                strip_unit(unit, False)
            upos += 5

        w2c = one.tile([P, C], U32, name="w2c", align_bytes=64)
        w2s = one.tile([P, C], U8, name="w2s", align_bytes=64)
        wu = two.tile([P, T, C], BF16, name="wu", tag="wrow", align_bytes=64)
        for t in range(T):
            nc.vector.tensor_tensor(out=wu[:, t, :], in0=wb[:, t, :].bitcast(FP8), in1=sc[:], op=ALU.mult)
        stationary(wu, w2c, w2s)

        ag = one.tile([P, H, W, T], BF16, name="ag", tag="raster", align_bytes=64)
        agflat = ag[:].rearrange("p h w t -> p (h w t)")
        agq = one.tile([P, NPIX], U32, name="agq", align_bytes=64)
        ags = one.tile([P, NPIX], U8, name="ags", align_bytes=64)
        outv = out.rearrange("o (p t) h w -> (o p) t (h w)", t=T)
        xflat = x.rearrange("o (p t) h w -> (o p) t (h w)", t=T)

        def finish(k):
            px = slice(CHUNK * k, CHUNK * (k + 1))
            res = two.tile([P, T, CHUNK], BF16, name="res")
            nc.sync.dma_start(out=res[:], in_=xflat[:, :, px])
            nc.vector.quantize_mx(
                out=agq[:, px].bitcast(FP8X4), scales=ags[:, px], in_=agflat[:, T * CHUNK * k : T * CHUNK * (k + 1)]
            )
            o = two.tile([P, T, CHUNK], F32, name="o")
            for half in (0, 1):
                ops = psum_out.tile([P, 2, CHUNK], F32, name="ops")
                for j in (0, 1):
                    t = 2 * half + j
                    nc.tensor.matmul_mx(
                        out=ops[:, j, :],
                        lhsT=w2c[:, P * t : P * t + P].bitcast(FP8X4),
                        lhsT_scale=w2s[:, P * t : P * t + P],
                        rhs=agq[:, px].bitcast(FP8X4),
                        rhs_scale=ags[:, px],
                        start=True,
                        stop=True,
                    )
                nc.vector.tensor_tensor(
                    out=o[:, 2 * half : 2 * half + 2, :], in0=ops[:], in1=res[:, 2 * half : 2 * half + 2, :], op=ALU.add
                )
            nc.sync.dma_start(out=outv[:, :, px], in_=o[:])

        nwin = 0
        nchunk = 0
        for wr in range(WROWS):
            nr = 4 if wr < 9 else 2
            for half in (0, 1):
                agg = psum_agg.tile([P, T, 4, 24], F32, name="agg", tag="agg")
                for q in range(4):
                    b = 4 * half + q
                    k, s = wr % 4, wr // 4
                    lscale = xbs[:, b, 48 * wr : 48 * wr + P] if k == 0 else xbk[k][:, b, s, :]
                    wps = psum_win.tile([P, C], F32, name="wps", tag="win")
                    nc.tensor.matmul_mx(
                        out=wps[:],
                        lhsT=xbq[:, b, 48 * wr : 48 * wr + P].bitcast(FP8X4),
                        lhsT_scale=lscale,
                        rhs=w1c[:].bitcast(FP8X4),
                        rhs_scale=w1s[:],
                        start=True,
                        stop=True,
                    )
                    ms = four.tile([P, C], F32, name="ms")
                    nc.scalar.copy(out=ms[:], in_=wps[:])
                    for t in range(T):
                        nc.tensor.matmul(
                            out=agg[:, t, 0:nr, 6 * q : 6 * q + 6],
                            lhsT=ms[:, P * t : P * t + P],
                            rhs=eg[:, wr, b, 0 : 6 * nr].rearrange("s (r c) -> s r c", c=6),
                            start=True,
                            stop=True,
                        )
                    nwin += 1
                    want = 30 + (len(units) - 30) * nwin // 72
                    while upos < min(want, len(units)):
                        strip_unit(units[upos], upos % 4 == 3)
                        upos += 1
                nc.scalar.copy(
                    out=ag[:, 4 * wr : 4 * wr + nr, 24 * half : 24 * half + 24, :],
                    in_=agg[:, :, 0:nr, :].rearrange("m t r c -> m r c t"),
                )
            while CHUNK * (nchunk + 1) <= W * (4 * wr + nr):
                finish(nchunk)
                nchunk += 1

        for e in range(4):
            nc.vector.tensor_tensor(out=acc[0][e][:], in0=acc[0][e][:], in1=acc[1][e][:], op=ALU.add)
            vt = psum_agg.tile([P, T, P], F32, name="vt", tag="agg")
            for t in range(T):
                nc.tensor.transpose(vt[:, t, :], acc[0][e][:, P * t : P * t + P], ident_f[:])
            if e < 3:
                nc.scalar.copy(
                    out=ag[:, 38:46, e:W:3, :], in_=vt[:].rearrange("m t (r c) -> m r c t", c=16)
                )
            else:
                nc.scalar.copy(
                    out=ag[:, 46:48, :, :], in_=vt[:].rearrange("m t (r c) -> m r c t", c=64)[:, :, 0:W, :]
                )
        for k in range(nchunk, NPIX // CHUNK):
            finish(k)
